import numpy as np
import ml_dtypes


def mxq(x, axis, fmt="e4m3"):
    dtype, down = {"e4m3": (ml_dtypes.float8_e4m3fn, 7), "e5m2": (ml_dtypes.float8_e5m2, 14)}[fmt]
    v = np.moveaxis(np.asarray(x, np.float32).astype(ml_dtypes.bfloat16).astype(np.float64), axis, -1)
    blocks = v.reshape(v.shape[:-1] + (-1, 32))
    amax = np.abs(blocks).max(-1, keepdims=True)
    byte = np.maximum(np.where(amax > 0, np.frexp(amax)[1] - 1 + 127, 0) - down, 1)
    scale = np.exp2(byte - 127.0)
    codes = (blocks / scale).astype(np.float32).astype(dtype).astype(np.float64)
    return np.moveaxis((codes * scale).reshape(v.shape), -1, axis)


WIDE = False


def mx_kscale(k):
    if not WIDE:
        return np.ones(k)
    levels = np.array([10, -10, 5, -5, 0])
    a = np.random.permutation(np.resize(levels, k // 512 * 4)).reshape(k // 512, 4)
    idx = np.arange(k)
    return np.exp2(a[idx // 512, idx % 128 // 32])


BF16 = ml_dtypes.bfloat16


def bf(x):
    return np.asarray(x, np.float32).astype(BF16)


def f64(x):
    return np.asarray(x).astype(np.float64)


E2M1 = np.array([0.0, 0.5, 1.0, 1.5, 2.0, 3.0, 4.0, 6.0, -0.0, -0.5, -1.0, -1.5, -2.0, -3.0, -4.0, -6.0])


def pack_weight(w, fmt):
    k, n = w.shape
    w = f64(bf(w)).reshape(k // 32, 32, n)
    amax = np.abs(w).max(1)
    if fmt == "e4m3":
        byte = np.frexp(amax)[1] - 1 + 127 - 7
    else:
        mant, ex = np.frexp(amax / 6.0)
        byte = np.where(mant > 0.5, ex, ex - 1) + 127
    byte = np.clip(np.where(amax > 0, byte, 1), 1, 254)
    scaled = (w * np.exp2(127.0 - byte)[:, None, :]).reshape(k, n).astype(np.float32)
    by_word = np.ascontiguousarray(scaled.reshape(k // 512, 128, 4, n).transpose(0, 1, 3, 2))
    if fmt == "e4m3":
        words = by_word.astype(ml_dtypes.float8_e4m3fn).view(np.uint8)
    else:
        c = by_word.astype(ml_dtypes.float4_e2m1fn).view(np.uint8) & 0xF
        words = c[..., 0::2] | (c[..., 1::2] << 4)
    return np.ascontiguousarray(words), np.ascontiguousarray(byte.astype(np.uint8).reshape(k // 512, 16, n))


def unpack_weight(words, scales, fmt):
    g, p, n, _ = words.shape
    if fmt == "e4m3":
        vals = np.ascontiguousarray(words).view(ml_dtypes.float8_e4m3fn).astype(np.float64)
    else:
        nib = np.empty((g, p, n, 4), np.uint8)
        nib[..., 0::2] = words & 0xF
        nib[..., 1::2] = words >> 4
        vals = E2M1[nib]
    vals = vals * np.repeat(np.exp2(scales.astype(np.float64) - 127.0), 8, axis=1)[..., None]
    return vals.transpose(0, 1, 3, 2).reshape(g * 512, n)


B, STACK, TUBE, CH, IMG, PATCH, EMBED = 4, 8, 4, 1, 128, 32, 4096
GH = IMG // PATCH
GW = IMG // PATCH
GD = STACK // TUBE
K = TUBE * CH * PATCH * PATCH


def _sincos_1d(dim, pos):
    omega = 1.0 / (10000.0 ** (np.arange(dim // 2, dtype=np.float64) / (dim / 2.0)))
    out = pos[:, None].astype(np.float64) * omega[None, :]
    return np.concatenate([np.sin(out), np.cos(out)], axis=1)


def get_3d_sincos_pos_embed(grid_h, grid_w, grid_depth, embed_dim):
    dim_t = embed_dim // 4
    dim_s = embed_dim - dim_t
    emb_t = _sincos_1d(dim_t, np.arange(grid_depth))
    emb_h = _sincos_1d(dim_s // 2, np.arange(grid_h))
    emb_w = _sincos_1d(dim_s - dim_s // 2, np.arange(grid_w))
    emb_hw = np.concatenate([np.repeat(emb_h, grid_w, axis=0), np.tile(emb_w, (grid_h, 1))], axis=1)
    ns = grid_h * grid_w
    return np.concatenate([np.repeat(emb_t, ns, axis=0), np.tile(emb_hw, (grid_depth, 1))], axis=1)


def setup_inputs():
    s = mx_kscale(K)
    sv = s.reshape(TUBE, CH, PATCH, PATCH)[:, :, None, :, None, :]
    video = np.random.standard_normal((B, GD, TUBE, CH, GH, PATCH, GW, PATCH)) * sv
    w_nk = np.random.standard_normal((EMBED, K)) / np.sqrt(K) / s[None, :]
    words, scales = pack_weight(np.ascontiguousarray(w_nk.T), "e4m3")
    return {"video": bf(video.reshape(B, STACK, CH, IMG, IMG)),
            "W_words": words,
            "W_scales": scales,
            "b": bf(np.random.standard_normal(EMBED) * 0.3),
            "pos_embed": bf(get_3d_sincos_pos_embed(GH, GW, GD, EMBED)[None])}


def reference(video, W_words, W_scales, b, pos_embed):
    video = f64(video)
    B_, T, C, H, W_ = video.shape
    p = PATCH
    gh, gw = H // p, W_ // p
    ns = gh * gw
    x = video.reshape(B_ * T, C, gh, p, gw, p)
    x = x.transpose(0, 2, 4, 1, 3, 5)
    x = x.reshape(B_, T, ns, C * p * p)
    x = x.reshape(B_, GD, TUBE, ns, C * p * p)
    x = x.transpose(0, 1, 3, 2, 4)
    tubelets = x.reshape(B_, GD * ns, TUBE * C * p * p)
    tokens = (mxq(tubelets, 2, "e4m3") @ unpack_weight(W_words, W_scales, "e4m3")) + f64(b) + f64(pos_embed)
    return tokens

@@ -1,0 +1,150 @@
+import concourse.mybir as mybir
+from concourse.masks import make_identity
+
+F32 = mybir.dt.float32
+BF16 = mybir.dt.bfloat16
+I32 = mybir.dt.int32
+U32 = mybir.dt.uint32
+U8 = mybir.dt.uint8
+FP8X4 = mybir.dt.float8_e4m3fn_x4
+
+P = 128
+PACK = 4
+K = 4096
+N = 4096
+GROUPS = K // (P * PACK)
+BANK = 512
+BANKS = N // BANK
+HALVES = 2
+FRAMES = 4
+GRID = 4
+TUBES = 8
+POS_ROWS = 32
+QUARTER = N // 4
+LIVE = 4
+PLANES = 4
+
+FLOPS = 2 * P * K * N
+
+
+def copy_words(nc, turn, out, in_):
+    if turn == 0:
+        nc.vector.tensor_copy(out=out, in_=in_)
+    else:
+        nc.scalar.copy(out=out, in_=in_)
+
+
+def tile_tubeletembedding_w_kernel(tc, video, W_words, W_scales, b, pos_embed, out):
+    nc = tc.nc
+    with tc.tile_pool(name="keep", bufs=1) as keep, tc.psum_pool(name="psum", bufs=BANKS) as psum:
+        w_words = keep.tile([P, GROUPS, N], U32, align_bytes=64)
+        w_planes = keep.tile([P, GROUPS // PLANES, N], U8, align_bytes=64)
+        x_codes = keep.tile([P, HALVES, FRAMES, P], U32, align_bytes=64)
+        x_scales = keep.tile([P, HALVES, FRAMES, P], U8, align_bytes=64)
+        tokens = keep.tile([P, N], F32)
+
+        nc.vector.memset(w_planes[:].bitcast(I32), 0)
+
+        pos_rows = keep.tile([P, QUARTER], BF16)
+        nc.sync.dma_start(out=pos_rows[:], in_=pos_embed.rearrange("o n (c w) -> (o n c) w", w=QUARTER))
+        b_rows = keep.tile([P, QUARTER], BF16)
+        nc.sync.dma_start(
+            out=b_rows[:],
+            in_=b.rearrange("(c w) -> c w", w=QUARTER).unsqueeze(0).to_broadcast([POS_ROWS, N // QUARTER, QUARTER]),
+        )
+        frames = keep.tile([P, K], BF16)
+        nc.sync.dma_start(out=frames[:], in_=video.rearrange("b f c (i y) x -> (b f c i) (y x)", i=GRID))
+        for s in range(GROUPS // PLANES):
+            for Q in range(4):
+                nc.sync.dma_start(
+                    out=w_planes[32 * Q : 32 * Q + LIVE * PLANES, s, :].bitcast(I32),
+                    in_=W_scales[PLANES * s : PLANES * (s + 1), LIVE * Q : LIVE * (Q + 1), :].bitcast(I32),
+                )
+        for g in range(GROUPS - 1):
+            nc.sync.dma_start(
+                out=w_words[:, g, :].bitcast(I32),
+                in_=W_words[g].rearrange("p n t -> p (n t)").bitcast(I32),
+            )
+        for nb in range(BANKS):
+            cols = slice(nb * BANK, (nb + 1) * BANK)
+            nc.sync.dma_start(
+                out=w_words[:, GROUPS - 1, cols].bitcast(I32),
+                in_=W_words[GROUPS - 1, :, cols, :].rearrange("p n t -> p (n t)").bitcast(I32),
+            )
+
+        ident = keep.tile([P, P], F32)
+        make_identity(nc, ident[:])
+        spread = keep.tile([P, N // QUARTER, P], BF16)
+        nc.vector.tensor_copy(
+            out=spread[:].rearrange("k c (a n) -> k c a n", n=POS_ROWS),
+            in_=ident[:]
+            .rearrange("k (n c) -> k c n", n=POS_ROWS)
+            .unsqueeze(2)
+            .to_broadcast([P, N // QUARTER, P // POS_ROWS, POS_ROWS]),
+        )
+        by_frame = keep.tile([P, P], F32)
+        nc.vector.tensor_copy(
+            out=by_frame[:].rearrange("q (s d i) -> q s d i", s=FRAMES, d=TUBES),
+            in_=ident[:].rearrange("q (d s i) -> q s d i", s=FRAMES, d=TUBES),
+        )
+
+        for nb in range(BANKS):
+            c = nb * BANK // QUARTER
+            cols = slice(nb * BANK - c * QUARTER, (nb + 1) * BANK - c * QUARTER)
+            addend = psum.tile([P, BANK], F32, tag="bank")
+            nc.tensor.matmul(addend[:], lhsT=spread[:, c, :], rhs=pos_rows[:, cols], start=True, stop=False)
+            nc.tensor.matmul(addend[:], lhsT=spread[:, c, :], rhs=b_rows[:, cols], start=False, stop=True)
+            copy_words(nc, nb % 2, out=tokens[:, nb * BANK : (nb + 1) * BANK], in_=addend[:])
+
+        sorted_words = keep.tile([P, HALVES, GRID, 2, P], F32)
+        frame_words = frames[:].bitcast(F32).rearrange(
+            "q (h y j c u) -> q h u j y c", h=HALVES, y=16, j=GRID, c=8, u=2
+        )
+        for h in range(HALVES):
+            for u in range(2):
+                copy_words(
+                    nc,
+                    h,
+                    out=sorted_words[:, h, :, u, :].rearrange("q j (y c) -> q j y c", c=8),
+                    in_=frame_words[:, h, u],
+                )
+        grouped = keep.tile([P, HALVES, FRAMES, P, PACK], BF16, align_bytes=64)
+        for h in range(HALVES):
+            grouped_words = grouped[:, h].bitcast(F32).rearrange("p s (r a l) u -> p s r a (l u)", a=2, l=2)
+            for a in range(GRID // 2):
+                turned = psum.tile([P, 4, P], F32, tag="bank")
+                for l in range(2):
+                    for u in range(2):
+                        nc.tensor.transpose(turned[:, 2 * l + u, :], sorted_words[:, h, 2 * a + l, u, :], by_frame[:])
+                copy_words(
+                    nc,
+                    h,
+                    out=grouped_words[:, :, :, a, :],
+                    in_=turned[:].rearrange("p w (s r) -> p s r w", s=FRAMES),
+                )
+        for h in range(HALVES):
+            nc.vector.quantize_mx(
+                out=x_codes[:, h].rearrange("p s m -> p (s m)").bitcast(FP8X4),
+                scales=x_scales[:, h].rearrange("p s m -> p (s m)"),
+                in_=grouped[:, h].rearrange("p s m t -> p (s m t)"),
+            )
+
+        sums = [psum.tile([P, BANK], F32, name="sums%d" % nb, tag="bank") for nb in range(BANKS)]
+        out_rows = out.rearrange("b n e -> (b n) e")
+        for g in range(GROUPS):
+            first_row = LIVE * (g % PLANES)
+            for nb in range(BANKS):
+                cols = slice(nb * BANK, (nb + 1) * BANK)
+                nc.tensor.matmul_mx(
+                    out=sums[nb][:],
+                    lhsT=x_codes[:, g % HALVES, g // HALVES, :].bitcast(FP8X4),
+                    lhsT_scale=x_scales[:, g % HALVES, g // HALVES, :],
+                    rhs=w_words[:, g, cols].bitcast(FP8X4),
+                    rhs_scale=w_planes[first_row:P, g // PLANES, cols],
+                    start=(g == 0),
+                    stop=(g == GROUPS - 1),
+                )
+        for nb in range(BANKS):
+            cols = slice(nb * BANK, (nb + 1) * BANK)
+            nc.vector.tensor_tensor(out=tokens[:, cols], in0=sums[nb][:], in1=tokens[:, cols], op=mybir.AluOpType.add)
+            nc.sync.dma_start(out=out_rows[:, cols], in_=tokens[:, cols])

@@ -43,17 +43,15 @@ def tile_tubeletembedding_w_kernel(tc, video, W_words, W_scales, b, pos_embed, o
         x_scales = keep.tile([P, HALVES, FRAMES, P], U8, align_bytes=64)
         tokens = keep.tile([P, N], F32)
 
+        b_rows = keep.tile([P, QUARTER], BF16)
+        nc.vector.memset(b_rows[:], 0.0)
         nc.vector.memset(w_planes[:].bitcast(I32), 0)
 
         pos_rows = keep.tile([P, QUARTER], BF16)
         nc.sync.dma_start(out=pos_rows[:], in_=pos_embed.rearrange("o n (c w) -> (o n c) w", w=QUARTER))
-        b_rows = keep.tile([P, QUARTER], BF16)
-        nc.sync.dma_start(
-            out=b_rows[:],
-            in_=b.rearrange("(c w) -> c w", w=QUARTER).unsqueeze(0).to_broadcast([POS_ROWS, N // QUARTER, QUARTER]),
-        )
         frames = keep.tile([P, K], BF16)
         nc.sync.dma_start(out=frames[:], in_=video.rearrange("b f c (i y) x -> (b f c i) (y x)", i=GRID))
+        nc.sync.dma_start(out=b_rows[0 : N // QUARTER, :], in_=b.rearrange("(c w) -> c w", w=QUARTER))
         for s in range(GROUPS // PLANES):
             for Q in range(4):
                 nc.sync.dma_start(
@@ -82,6 +80,10 @@ def tile_tubeletembedding_w_kernel(tc, video, W_words, W_scales, b, pos_embed, o
             .unsqueeze(2)
             .to_broadcast([P, N // QUARTER, P // POS_ROWS, POS_ROWS]),
         )
+        pick = keep.tile([P, N // QUARTER, P], BF16)
+        nc.vector.tensor_copy(
+            out=pick[:], in_=ident[:, 0 : N // QUARTER].unsqueeze(2).to_broadcast([P, N // QUARTER, P])
+        )
         by_frame = keep.tile([P, P], F32)
         nc.vector.tensor_copy(
             out=by_frame[:].rearrange("q (s d i) -> q s d i", s=FRAMES, d=TUBES),
@@ -93,7 +95,7 @@ def tile_tubeletembedding_w_kernel(tc, video, W_words, W_scales, b, pos_embed, o
             cols = slice(nb * BANK - c * QUARTER, (nb + 1) * BANK - c * QUARTER)
             addend = psum.tile([P, BANK], F32, tag="bank")
             nc.tensor.matmul(addend[:], lhsT=spread[:, c, :], rhs=pos_rows[:, cols], start=True, stop=False)
-            nc.tensor.matmul(addend[:], lhsT=spread[:, c, :], rhs=b_rows[:, cols], start=False, stop=True)
+            nc.tensor.matmul(addend[:], lhsT=pick[:, c, :], rhs=b_rows[:, cols], start=False, stop=True)
             copy_words(nc, nb % 2, out=tokens[:, nb * BANK : (nb + 1) * BANK], in_=addend[:])
 
         sorted_words = keep.tile([P, HALVES, GRID, 2, P], F32)

@@ -133,19 +133,20 @@ def tile_tubeletembedding_w_kernel(tc, video, W_words, W_scales, b, pos_embed, o
 
         sums = [psum.tile([P, BANK], F32, name="sums%d" % nb, tag="bank") for nb in range(BANKS)]
         out_rows = out.rearrange("b n e -> (b n) e")
-        for g in range(GROUPS):
+        passes = [(g, nb) for g in range(GROUPS - 2) for nb in range(BANKS)]
+        passes += [(g, nb) for nb in range(BANKS) for g in (GROUPS - 2, GROUPS - 1)]
+        for g, nb in passes:
             first_row = LIVE * (g % PLANES)
-            for nb in range(BANKS):
-                cols = slice(nb * BANK, (nb + 1) * BANK)
-                nc.tensor.matmul_mx(
-                    out=sums[nb][:],
-                    lhsT=x_codes[:, g % HALVES, g // HALVES, :].bitcast(FP8X4),
-                    lhsT_scale=x_scales[:, g % HALVES, g // HALVES, :],
-                    rhs=w_words[:, g, cols].bitcast(FP8X4),
-                    rhs_scale=w_planes[first_row:P, g // PLANES, cols],
-                    start=(g == 0),
-                    stop=(g == GROUPS - 1),
-                )
+            cols = slice(nb * BANK, (nb + 1) * BANK)
+            nc.tensor.matmul_mx(
+                out=sums[nb][:],
+                lhsT=x_codes[:, g % HALVES, g // HALVES, :].bitcast(FP8X4),
+                lhsT_scale=x_scales[:, g % HALVES, g // HALVES, :],
+                rhs=w_words[:, g, cols].bitcast(FP8X4),
+                rhs_scale=w_planes[first_row:P, g // PLANES, cols],
+                start=(g == 0),
+                stop=(g == GROUPS - 1),
+            )
         for nb in range(BANKS):
             cols = slice(nb * BANK, (nb + 1) * BANK)
             nc.vector.tensor_tensor(out=tokens[:, cols], in0=sums[nb][:], in1=tokens[:, cols], op=mybir.AluOpType.add)

@@ -24,6 +24,9 @@ QUARTER = N // 4
 LIVE = 4
 PLANES = 4
 
+LAST_LOADS = ((6, 0, 4), (7, 0, 4), (6, 4, 4), (7, 4, 2), (7, 6, 1), (7, 7, 1))
+STORES = ((0, 2), (2, 2), (4, 2), (6, 1), (7, 1))
+
 FLOPS = 2 * P * K * N
 
 
@@ -58,16 +61,16 @@ def tile_tubeletembedding_w_kernel(tc, video, W_words, W_scales, b, pos_embed, o
                     out=w_planes[32 * Q : 32 * Q + LIVE * PLANES, s, :].bitcast(I32),
                     in_=W_scales[PLANES * s : PLANES * (s + 1), LIVE * Q : LIVE * (Q + 1), :].bitcast(I32),
                 )
-        for g in range(GROUPS - 1):
+        for g in range(GROUPS - 2):
             nc.sync.dma_start(
                 out=w_words[:, g, :].bitcast(I32),
                 in_=W_words[g].rearrange("p n t -> p (n t)").bitcast(I32),
             )
-        for nb in range(BANKS):
-            cols = slice(nb * BANK, (nb + 1) * BANK)
+        for g, first_bank, banks in LAST_LOADS:
+            cols = slice(first_bank * BANK, (first_bank + banks) * BANK)
             nc.sync.dma_start(
-                out=w_words[:, GROUPS - 1, cols].bitcast(I32),
-                in_=W_words[GROUPS - 1, :, cols, :].rearrange("p n t -> p (n t)").bitcast(I32),
+                out=w_words[:, g, cols].bitcast(I32),
+                in_=W_words[g, :, cols, :].rearrange("p n t -> p (n t)").bitcast(I32),
             )
 
         ident = keep.tile([P, P], F32)
@@ -134,7 +137,7 @@ def tile_tubeletembedding_w_kernel(tc, video, W_words, W_scales, b, pos_embed, o
         sums = [psum.tile([P, BANK], F32, name="sums%d" % nb, tag="bank") for nb in range(BANKS)]
         out_rows = out.rearrange("b n e -> (b n) e")
         passes = [(g, nb) for g in range(GROUPS - 2) for nb in range(BANKS)]
-        passes += [(g, nb) for nb in range(BANKS) for g in (GROUPS - 2, GROUPS - 1)]
+        passes += [(g, nb) for g, first_bank, banks in LAST_LOADS for nb in range(first_bank, first_bank + banks)]
         for g, nb in passes:
             first_row = LIVE * (g % PLANES)
             cols = slice(nb * BANK, (nb + 1) * BANK)
@@ -147,7 +150,11 @@ def tile_tubeletembedding_w_kernel(tc, video, W_words, W_scales, b, pos_embed, o
                 start=(g == 0),
                 stop=(g == GROUPS - 1),
             )
-        for nb in range(BANKS):
-            cols = slice(nb * BANK, (nb + 1) * BANK)
-            nc.vector.tensor_tensor(out=tokens[:, cols], in0=sums[nb][:], in1=tokens[:, cols], op=mybir.AluOpType.add)
+        for first_bank, banks in STORES:
+            for nb in range(first_bank, first_bank + banks):
+                cols = slice(nb * BANK, (nb + 1) * BANK)
+                nc.vector.tensor_tensor(
+                    out=tokens[:, cols], in0=sums[nb][:], in1=tokens[:, cols], op=mybir.AluOpType.add
+                )
+            cols = slice(first_bank * BANK, (first_bank + banks) * BANK)
             nc.sync.dma_start(out=out_rows[:, cols], in_=tokens[:, cols])

@@ -55,12 +55,15 @@ def tile_tubeletembedding_w_kernel(tc, video, W_words, W_scales, b, pos_embed, o
         frames = keep.tile([P, K], BF16)
         nc.sync.dma_start(out=frames[:], in_=video.rearrange("b f c (i y) x -> (b f c i) (y x)", i=GRID))
         nc.sync.dma_start(out=b_rows[0 : N // QUARTER, :], in_=b.rearrange("(c w) -> c w", w=QUARTER))
-        for s in range(GROUPS // PLANES):
-            for Q in range(4):
-                nc.sync.dma_start(
-                    out=w_planes[32 * Q : 32 * Q + LIVE * PLANES, s, :].bitcast(I32),
-                    in_=W_scales[PLANES * s : PLANES * (s + 1), LIVE * Q : LIVE * (Q + 1), :].bitcast(I32),
-                )
+        for Q in range(4):
+            nc.sync.dma_start(
+                out=w_planes[32 * Q : 32 * Q + LIVE * PLANES, 0, :].bitcast(I32),
+                in_=W_scales[0:PLANES, LIVE * Q : LIVE * (Q + 1), :].bitcast(I32),
+            )
+            nc.gpsimd.dma_start(
+                out=w_planes[32 * Q : 32 * Q + LIVE * PLANES, 1, :].bitcast(F32),
+                in_=W_scales[PLANES : 2 * PLANES, LIVE * Q : LIVE * (Q + 1), :].bitcast(F32),
+            )
         for g in range(GROUPS - 2):
             nc.sync.dma_start(
                 out=w_words[:, g, :].bitcast(I32),

@@ -54,6 +54,9 @@ def tile_tubeletembedding_w_kernel(tc, video, W_words, W_scales, b, pos_embed, o
         nc.sync.dma_start(out=pos_rows[:], in_=pos_embed.rearrange("o n (c w) -> (o n c) w", w=QUARTER))
         frames = keep.tile([P, K], BF16)
         nc.sync.dma_start(out=frames[:], in_=video.rearrange("b f c (i y) x -> (b f c i) (y x)", i=GRID))
+        nc.sync.dma_start(
+            out=w_words[:, 0, :].bitcast(I32), in_=W_words[0].rearrange("p n t -> p (n t)").bitcast(I32)
+        )
         nc.sync.dma_start(out=b_rows[0 : N // QUARTER, :], in_=b.rearrange("(c w) -> c w", w=QUARTER))
         for Q in range(4):
             nc.sync.dma_start(
@@ -64,7 +67,7 @@ def tile_tubeletembedding_w_kernel(tc, video, W_words, W_scales, b, pos_embed, o
                 out=w_planes[32 * Q : 32 * Q + LIVE * PLANES, 1, :].bitcast(F32),
                 in_=W_scales[PLANES : 2 * PLANES, LIVE * Q : LIVE * (Q + 1), :].bitcast(F32),
             )
-        for g in range(GROUPS - 2):
+        for g in range(1, GROUPS - 2):
             nc.sync.dma_start(
                 out=w_words[:, g, :].bitcast(I32),
                 in_=W_words[g].rearrange("p n t -> p (n t)").bitcast(I32),

@@ -57,16 +57,23 @@ def tile_tubeletembedding_w_kernel(tc, video, W_words, W_scales, b, pos_embed, o
         nc.sync.dma_start(
             out=w_words[:, 0, :].bitcast(I32), in_=W_words[0].rearrange("p n t -> p (n t)").bitcast(I32)
         )
-        nc.sync.dma_start(out=b_rows[0 : N // QUARTER, :], in_=b.rearrange("(c w) -> c w", w=QUARTER))
         for Q in range(4):
             nc.sync.dma_start(
                 out=w_planes[32 * Q : 32 * Q + LIVE * PLANES, 0, :].bitcast(I32),
                 in_=W_scales[0:PLANES, LIVE * Q : LIVE * (Q + 1), :].bitcast(I32),
             )
-            nc.gpsimd.dma_start(
-                out=w_planes[32 * Q : 32 * Q + LIVE * PLANES, 1, :].bitcast(F32),
-                in_=W_scales[PLANES : 2 * PLANES, LIVE * Q : LIVE * (Q + 1), :].bitcast(F32),
-            )
+        b_quarters = b.rearrange("(c w) -> c w", w=QUARTER)
+        with tc.manual_schedule(engines={mybir.EngineType.Pool}):
+            for turn in range(2 * PLANES):
+                if turn % PLANES == 0:
+                    half = slice(turn // PLANES * (QUARTER // 2), (turn // PLANES + 1) * (QUARTER // 2))
+                    nc.gpsimd.dma_start(out=b_rows[0 : N // QUARTER, half], in_=b_quarters[:, half])
+                elif turn - turn // PLANES <= PLANES:
+                    Q = turn - turn // PLANES - 1
+                    nc.gpsimd.dma_start(
+                        out=w_planes[32 * Q : 32 * Q + LIVE * PLANES, 1, :].bitcast(F32),
+                        in_=W_scales[PLANES : 2 * PLANES, LIVE * Q : LIVE * (Q + 1), :].bitcast(F32),
+                    )
         for g in range(1, GROUPS - 2):
             nc.sync.dma_start(
                 out=w_words[:, g, :].bitcast(I32),

import concourse.mybir as mybir
from concourse.masks import make_identity

F32 = mybir.dt.float32
BF16 = mybir.dt.bfloat16
I32 = mybir.dt.int32
U32 = mybir.dt.uint32
U8 = mybir.dt.uint8
FP8X4 = mybir.dt.float8_e4m3fn_x4

P = 128
PACK = 4
K = 4096
N = 4096
GROUPS = K // (P * PACK)
BANK = 512
BANKS = N // BANK
HALVES = 2
FRAMES = 4
GRID = 4
TUBES = 8
POS_ROWS = 32
QUARTER = N // 4
LIVE = 4
PLANES = 4

LAST_LOADS = ((6, 0, 4), (7, 0, 4), (6, 4, 4), (7, 4, 2), (7, 6, 1), (7, 7, 1))
STORES = ((0, 2), (2, 2), (4, 2), (6, 1), (7, 1))

FLOPS = 2 * P * K * N


def copy_words(nc, turn, out, in_):
    if turn == 0:
        nc.vector.tensor_copy(out=out, in_=in_)
    else:
        nc.scalar.copy(out=out, in_=in_)


def tile_tubeletembedding_w_kernel(tc, video, W_words, W_scales, b, pos_embed, out):
    nc = tc.nc
    with tc.tile_pool(name="keep", bufs=1) as keep, tc.psum_pool(name="psum", bufs=BANKS) as psum:
        w_words = keep.tile([P, GROUPS, N], U32, align_bytes=64)
        w_planes = keep.tile([P, GROUPS // PLANES, N], U8, align_bytes=64)
        x_codes = keep.tile([P, HALVES, FRAMES, P], U32, align_bytes=64)
        x_scales = keep.tile([P, HALVES, FRAMES, P], U8, align_bytes=64)
        tokens = keep.tile([P, N], F32)

        b_rows = keep.tile([P, QUARTER], BF16)
        nc.vector.memset(b_rows[:], 0.0)
        nc.vector.memset(w_planes[:].bitcast(I32), 0)

        pos_rows = keep.tile([P, QUARTER], BF16)
        nc.sync.dma_start(out=pos_rows[:], in_=pos_embed.rearrange("o n (c w) -> (o n c) w", w=QUARTER))
        frames = keep.tile([P, K], BF16)
        nc.sync.dma_start(out=frames[:], in_=video.rearrange("b f c (i y) x -> (b f c i) (y x)", i=GRID))
        nc.sync.dma_start(
            out=w_words[:, 0, :].bitcast(I32), in_=W_words[0].rearrange("p n t -> p (n t)").bitcast(I32)
        )
        for Q in range(4):
            nc.sync.dma_start(
                out=w_planes[32 * Q : 32 * Q + LIVE * PLANES, 0, :].bitcast(I32),
                in_=W_scales[0:PLANES, LIVE * Q : LIVE * (Q + 1), :].bitcast(I32),
            )
        b_quarters = b.rearrange("(c w) -> c w", w=QUARTER)
        with tc.manual_schedule(engines={mybir.EngineType.Pool}):
            for turn in range(2 * PLANES):
                if turn % PLANES == 0:
                    half = slice(turn // PLANES * (QUARTER // 2), (turn // PLANES + 1) * (QUARTER // 2))
                    nc.gpsimd.dma_start(out=b_rows[0 : N // QUARTER, half], in_=b_quarters[:, half])
                elif turn - turn // PLANES <= PLANES:
                    Q = turn - turn // PLANES - 1
                    nc.gpsimd.dma_start(
                        out=w_planes[32 * Q : 32 * Q + LIVE * PLANES, 1, :].bitcast(F32),
                        in_=W_scales[PLANES : 2 * PLANES, LIVE * Q : LIVE * (Q + 1), :].bitcast(F32),
                    )
        for g in range(1, GROUPS - 2):
            nc.sync.dma_start(
                out=w_words[:, g, :].bitcast(I32),
                in_=W_words[g].rearrange("p n t -> p (n t)").bitcast(I32),
            )
        for g, first_bank, banks in LAST_LOADS:
            cols = slice(first_bank * BANK, (first_bank + banks) * BANK)
            nc.sync.dma_start(
                out=w_words[:, g, cols].bitcast(I32),
                in_=W_words[g, :, cols, :].rearrange("p n t -> p (n t)").bitcast(I32),
            )

        ident = keep.tile([P, P], F32)
        make_identity(nc, ident[:])
        spread = keep.tile([P, N // QUARTER, P], BF16)
        nc.vector.tensor_copy(
            out=spread[:].rearrange("k c (a n) -> k c a n", n=POS_ROWS),
            in_=ident[:]
            .rearrange("k (n c) -> k c n", n=POS_ROWS)
            .unsqueeze(2)
            .to_broadcast([P, N // QUARTER, P // POS_ROWS, POS_ROWS]),
        )
        pick = keep.tile([P, N // QUARTER, P], BF16)
        nc.vector.tensor_copy(
            out=pick[:], in_=ident[:, 0 : N // QUARTER].unsqueeze(2).to_broadcast([P, N // QUARTER, P])
        )
        by_frame = keep.tile([P, P], F32)
        nc.vector.tensor_copy(
            out=by_frame[:].rearrange("q (s d i) -> q s d i", s=FRAMES, d=TUBES),
            in_=ident[:].rearrange("q (d s i) -> q s d i", s=FRAMES, d=TUBES),
        )

        for nb in range(BANKS):
            c = nb * BANK // QUARTER
            cols = slice(nb * BANK - c * QUARTER, (nb + 1) * BANK - c * QUARTER)
            addend = psum.tile([P, BANK], F32, tag="bank")
            nc.tensor.matmul(addend[:], lhsT=spread[:, c, :], rhs=pos_rows[:, cols], start=True, stop=False)
            nc.tensor.matmul(addend[:], lhsT=pick[:, c, :], rhs=b_rows[:, cols], start=False, stop=True)
            copy_words(nc, nb % 2, out=tokens[:, nb * BANK : (nb + 1) * BANK], in_=addend[:])

        sorted_words = keep.tile([P, HALVES, GRID, 2, P], F32)
        frame_words = frames[:].bitcast(F32).rearrange(
            "q (h y j c u) -> q h u j y c", h=HALVES, y=16, j=GRID, c=8, u=2
        )
        for h in range(HALVES):
            for u in range(2):
                copy_words(
                    nc,
                    h,
                    out=sorted_words[:, h, :, u, :].rearrange("q j (y c) -> q j y c", c=8),
                    in_=frame_words[:, h, u],
                )
        grouped = keep.tile([P, HALVES, FRAMES, P, PACK], BF16, align_bytes=64)
        for h in range(HALVES):
            grouped_words = grouped[:, h].bitcast(F32).rearrange("p s (r a l) u -> p s r a (l u)", a=2, l=2)
            for a in range(GRID // 2):
                turned = psum.tile([P, 4, P], F32, tag="bank")
                for l in range(2):
                    for u in range(2):
                        nc.tensor.transpose(turned[:, 2 * l + u, :], sorted_words[:, h, 2 * a + l, u, :], by_frame[:])
                copy_words(
                    nc,
                    h,
                    out=grouped_words[:, :, :, a, :],
                    in_=turned[:].rearrange("p w (s r) -> p s r w", s=FRAMES),
                )
        for h in range(HALVES):
            nc.vector.quantize_mx(
                out=x_codes[:, h].rearrange("p s m -> p (s m)").bitcast(FP8X4),
                scales=x_scales[:, h].rearrange("p s m -> p (s m)"),
                in_=grouped[:, h].rearrange("p s m t -> p (s m t)"),
            )

        sums = [psum.tile([P, BANK], F32, name="sums%d" % nb, tag="bank") for nb in range(BANKS)]
        out_rows = out.rearrange("b n e -> (b n) e")
        passes = [(g, nb) for g in range(GROUPS - 2) for nb in range(BANKS)]
        passes += [(g, nb) for g, first_bank, banks in LAST_LOADS for nb in range(first_bank, first_bank + banks)]
        for g, nb in passes:
            first_row = LIVE * (g % PLANES)
            cols = slice(nb * BANK, (nb + 1) * BANK)
            nc.tensor.matmul_mx(
                out=sums[nb][:],
                lhsT=x_codes[:, g % HALVES, g // HALVES, :].bitcast(FP8X4),
                lhsT_scale=x_scales[:, g % HALVES, g // HALVES, :],
                rhs=w_words[:, g, cols].bitcast(FP8X4),
                rhs_scale=w_planes[first_row:P, g // PLANES, cols],
                start=(g == 0),
                stop=(g == GROUPS - 1),
            )
        for first_bank, banks in STORES:
            for nb in range(first_bank, first_bank + banks):
                cols = slice(nb * BANK, (nb + 1) * BANK)
                nc.vector.tensor_tensor(
                    out=tokens[:, cols], in0=sums[nb][:], in1=tokens[:, cols], op=mybir.AluOpType.add
                )
            cols = slice(first_bank * BANK, (first_bank + banks) * BANK)
            nc.sync.dma_start(out=out_rows[:, cols], in_=tokens[:, cols])
